import numpy as np
import ml_dtypes


def mxq(x, axis, fmt="e4m3"):
    dtype, down = {"e4m3": (ml_dtypes.float8_e4m3fn, 7), "e5m2": (ml_dtypes.float8_e5m2, 14)}[fmt]
    v = np.moveaxis(np.asarray(x, np.float32).astype(ml_dtypes.bfloat16).astype(np.float64), axis, -1)
    blocks = v.reshape(v.shape[:-1] + (-1, 32))
    amax = np.abs(blocks).max(-1, keepdims=True)
    byte = np.maximum(np.where(amax > 0, np.frexp(amax)[1] - 1 + 127, 0) - down, 1)
    scale = np.exp2(byte - 127.0)
    codes = (blocks / scale).astype(np.float32).astype(dtype).astype(np.float64)
    return np.moveaxis((codes * scale).reshape(v.shape), -1, axis)


WIDE = False


def mx_kscale(k):
    if not WIDE:
        return np.ones(k)
    levels = np.array([10, -10, 5, -5, 0])
    a = np.random.permutation(np.resize(levels, k // 512 * 4)).reshape(k // 512, 4)
    idx = np.arange(k)
    return np.exp2(a[idx // 512, idx % 128 // 32])


BF16 = ml_dtypes.bfloat16


def bf(x):
    return np.asarray(x, np.float32).astype(BF16)


def f64(x):
    return np.asarray(x).astype(np.float64)


E2M1 = np.array([0.0, 0.5, 1.0, 1.5, 2.0, 3.0, 4.0, 6.0, -0.0, -0.5, -1.0, -1.5, -2.0, -3.0, -4.0, -6.0])


def pack_weight(w, fmt):
    k, n = w.shape
    w = f64(bf(w)).reshape(k // 32, 32, n)
    amax = np.abs(w).max(1)
    if fmt == "e4m3":
        byte = np.frexp(amax)[1] - 1 + 127 - 7
    else:
        mant, ex = np.frexp(amax / 6.0)
        byte = np.where(mant > 0.5, ex, ex - 1) + 127
    byte = np.clip(np.where(amax > 0, byte, 1), 1, 254)
    scaled = (w * np.exp2(127.0 - byte)[:, None, :]).reshape(k, n).astype(np.float32)
    by_word = np.ascontiguousarray(scaled.reshape(k // 512, 128, 4, n).transpose(0, 1, 3, 2))
    if fmt == "e4m3":
        words = by_word.astype(ml_dtypes.float8_e4m3fn).view(np.uint8)
    else:
        c = by_word.astype(ml_dtypes.float4_e2m1fn).view(np.uint8) & 0xF
        words = c[..., 0::2] | (c[..., 1::2] << 4)
    return np.ascontiguousarray(words), np.ascontiguousarray(byte.astype(np.uint8).reshape(k // 512, 16, n))


def unpack_weight(words, scales, fmt):
    g, p, n, _ = words.shape
    if fmt == "e4m3":
        vals = np.ascontiguousarray(words).view(ml_dtypes.float8_e4m3fn).astype(np.float64)
    else:
        nib = np.empty((g, p, n, 4), np.uint8)
        nib[..., 0::2] = words & 0xF
        nib[..., 1::2] = words >> 4
        vals = E2M1[nib]
    vals = vals * np.repeat(np.exp2(scales.astype(np.float64) - 127.0), 8, axis=1)[..., None]
    return vals.transpose(0, 1, 3, 2).reshape(g * 512, n)

def pack4(w):
    words, scales = pack_weight(w, "e2m1")
    return words.reshape(words.shape[0], 128, -1), scales


def unpack4(words, scales):
    return unpack_weight(words.reshape(words.shape[0], 128, -1, 2), scales, "e2m1")


B, N, D1, D2, F1, F2, F3, F4 = 1024, 1, 4096, 4096, 128, 64, 32, 16
K = D1 + D2
EPS = 1e-5
SLOPE = 0.2


def setup_inputs():
    s = mx_kscale(K)
    g = np.sqrt(EPS)
    input1 = bf(np.random.standard_normal((B, N, D1)) * s[:D1])
    input2 = bf(np.random.standard_normal((B, N, D2)) * s[D1:])
    w1 = np.random.standard_normal((F1, K)) * 5.0 * g / np.sqrt(K) / s[None, :]
    words, scales = pack4(np.ascontiguousarray(w1.T))
    b1 = bf(np.random.standard_normal(F1) * 2.5 * g)
    return {"input1": input1,
            "input2": input2,
            "W1_words": words,
            "W1_scales": scales,
            "b1": b1}


def reference(input1, input2, W1_words, W1_scales, b1):
    x = np.concatenate([f64(input1), f64(input2)], axis=2)
    h = (mxq(x, 2, "e4m3") @ unpack4(W1_words, W1_scales)) + f64(b1)
    m = h.mean(axis=-1, keepdims=True)
    v = np.square(h - m).mean(axis=-1, keepdims=True)
    hn = (h - m) * (1.0 / np.sqrt(v + EPS))
    return np.where(hn >= 0, hn, SLOPE * hn)

@@ -1,0 +1,194 @@
+import concourse.mybir as mybir
+from concourse.masks import make_identity
+
+F32 = mybir.dt.float32
+BF16 = mybir.dt.bfloat16
+I32 = mybir.dt.int32
+U32 = mybir.dt.uint32
+U8 = mybir.dt.uint8
+FP8X4 = mybir.dt.float8_e4m3fn_x4
+FP4X4 = mybir.dt.float4_e2m1fn_x4
+ALU = mybir.AluOpType
+ACT = mybir.ActivationFunctionType
+
+P = 128
+PACK = 4
+K_PASS = P * PACK
+ROWS = 1024
+K_INPUT = 4096
+FEATURES = 128
+EPS = 1e-5
+SLOPE = 0.2
+
+ROW_TILES = ROWS // P
+INPUTS = 2
+CHUNKS = ROW_TILES * INPUTS
+GROUPS = K_INPUT // K_PASS
+ALL_GROUPS = GROUPS * INPUTS
+WORDS = K_PASS // 2
+HALVES = 2
+BANK_GROUPS = 2
+QUANT_GROUPS = 4
+HEAD_PIECES = 4
+
+FLOPS = 2 * ROWS * K_INPUT * INPUTS * FEATURES
+
+
+def tile_fcd_pa_k_kernel(tc, input1, input2, W1_words, W1_scales, b1, out):
+    nc = tc.nc
+    x_rows = [
+        source.rearrange("(i p) o k -> i p (o k)", p=P) for source in (input1, input2)
+    ]
+    out_rows = out.rearrange("(i p) o f -> i p (o f)", p=P)
+
+    with tc.tile_pool(name="const", bufs=1) as const, tc.tile_pool(
+        name="resident", bufs=CHUNKS
+    ) as resident, tc.tile_pool(name="stage", bufs=3) as stage, tc.tile_pool(
+        name="norm", bufs=2
+    ) as norm, tc.psum_pool(name="flipped", bufs=6) as flipped, tc.psum_pool(
+        name="sums", bufs=2
+    ) as sums, tc.manual_schedule():
+        w_planes = const.tile([P, ALL_GROUPS, FEATURES], U8, align_bytes=64)
+        nc.vector.memset(w_planes[:].bitcast(I32), 0)
+        bias_row = const.tile([P, FEATURES], BF16)
+        nc.vector.memset(bias_row[:], 0.0)
+        ones = const.tile([P, P], BF16)
+        nc.vector.memset(ones[:], 1.0)
+        one = const.tile([P, 1], F32)
+        nc.vector.memset(one[:], 1.0)
+        identity = const.tile([P, P], F32)
+        make_identity(nc, identity[:])
+
+        nc.scalar.dma_start(out=bias_row[0:1, :], in_=b1.rearrange("(o f) -> o f", o=1))
+        warm = const.tile([P, 1], F32)
+        nc.scalar.activation(out=warm[:], in_=one[:], func=ACT.Sqrt)
+
+        w_words = const.tile([P, ALL_GROUPS, 2 * FEATURES], U8, align_bytes=64)
+        x_chunks = []
+        for c in range(CHUNKS):
+            x_sb = resident.tile([P, K_INPUT], BF16, name="x_sb")
+            x_chunks.append(x_sb)
+            source = x_rows[c % INPUTS][c // INPUTS]
+            pieces = HEAD_PIECES if c == 0 else 1
+            width = K_INPUT // pieces
+            for piece in range(pieces):
+                cols = slice(piece * width, (piece + 1) * width)
+                nc.sync.dma_start(out=x_sb[:, cols], in_=source[:, cols])
+            if c == 1:
+                for quadrant in range(4):
+                    nc.sync.dma_start(
+                        out=w_planes[32 * quadrant : 32 * quadrant + 4, :, :].bitcast(I32),
+                        in_=W1_scales[:, 4 * quadrant : 4 * quadrant + 4, :]
+                        .rearrange("g q n -> q g n")
+                        .bitcast(I32),
+                    )
+                nc.sync.dma_start(
+                    out=w_words[:].bitcast(I32),
+                    in_=W1_words.rearrange("g p c -> p g c").bitcast(I32),
+                )
+
+        bias_ps = flipped.tile([P, BANK_GROUPS, HALVES, P], F32, tag="bank")
+        nc.tensor.matmul(
+            out=bias_ps[:, 0, 0, :], lhsT=ones[:], rhs=bias_row[:], start=True, stop=True
+        )
+        bias_all = const.tile([P, FEATURES], F32)
+        nc.vector.tensor_copy(out=bias_all[:], in_=bias_ps[:, 0, 0, :])
+
+        grouped_of = {}
+        codes_of = {}
+        sum_of = {}
+        h_of = {}
+
+        def transpose_chunk(c):
+            x_words = x_chunks[c][:].bitcast(F32)
+            grouped = stage.tile([P, GROUPS, P, PACK], BF16, name="grouped", align_bytes=64)
+            grouped_of[c] = grouped
+            grouped_words = grouped[:].bitcast(F32)
+            for first in range(0, GROUPS, BANK_GROUPS):
+                bank = flipped.tile([P, BANK_GROUPS, HALVES, P], F32, name="bank", tag="bank")
+                for j in range(BANK_GROUPS):
+                    start_word = (first + j) * WORDS
+                    for u in range(HALVES):
+                        nc.tensor.transpose(
+                            bank[:, j, u, :],
+                            x_words[:, start_word + u : start_word + WORDS : HALVES],
+                            identity[:],
+                        )
+                nc.scalar.copy(
+                    out=grouped_words[:, first : first + BANK_GROUPS, :, :],
+                    in_=bank[:].rearrange("p g u r -> p g r u"),
+                )
+
+        def quantise_chunk(c):
+            grouped = grouped_of[c]
+            codes = stage.tile([P, GROUPS, P], U32, name="codes", align_bytes=64)
+            planes = stage.tile([P, GROUPS, P], U8, name="planes", align_bytes=64)
+            codes_of[c] = (codes, planes)
+            for first in range(0, GROUPS, QUANT_GROUPS):
+                some = slice(first, first + QUANT_GROUPS)
+                nc.vector.quantize_mx(
+                    out=codes[:, some, :].rearrange("p g r -> p (g r)").bitcast(FP8X4),
+                    scales=planes[:, some, :].rearrange("p g r -> p (g r)"),
+                    in_=grouped[:, some, :, :].rearrange("p g r t -> p (g r t)"),
+                )
+
+        def multiply_chunk(c):
+            codes, planes = codes_of[c]
+            if c % INPUTS == 0:
+                sum_of[c // INPUTS] = sums.tile([P, FEATURES], F32, name="total")
+            total = sum_of[c // INPUTS]
+            for g in range(GROUPS):
+                w_group = (c % INPUTS) * GROUPS + g
+                nc.tensor.matmul_mx(
+                    out=total[:],
+                    lhsT=codes[:, g, :].bitcast(FP8X4),
+                    lhsT_scale=planes[:, g, :],
+                    rhs=w_words[:, w_group, :].bitcast(FP4X4),
+                    rhs_scale=w_planes[:, w_group, :],
+                    start=(w_group == 0),
+                    stop=(w_group == ALL_GROUPS - 1),
+                )
+
+        def norm_statistics(i):
+            h = norm.tile([P, FEATURES], F32, name="h")
+            nc.vector.tensor_tensor(out=h[:], in0=sum_of[i][:], in1=bias_all[:], op=ALU.add)
+            stats = norm.tile([P, 6], F32, name="stats")
+            nc.vector.bn_stats(out=stats[:], in_=h[:])
+            mean_var = norm.tile([P, 2], F32, name="mean_var")
+            nc.vector.bn_aggr(out=mean_var[:], in_=stats[:])
+            shifted = norm.tile([P, 1], F32, name="shifted")
+            nc.vector.tensor_scalar_add(out=shifted[:], in0=mean_var[:, 1:2], scalar1=EPS)
+            deviation = norm.tile([P, 1], F32, name="deviation")
+            nc.scalar.activation(out=deviation[:], in_=shifted[:], func=ACT.Sqrt)
+            h_of[i] = (h, mean_var, deviation)
+
+        def norm_apply(i):
+            h, mean_var, deviation = h_of[i]
+            inverse = norm.tile([P, 1], F32, name="inverse")
+            nc.vector.reciprocal(out=inverse[:], in_=deviation[:])
+            hn = norm.tile([P, FEATURES], F32, name="hn")
+            nc.vector.tensor_scalar(
+                out=hn[:],
+                in0=h[:],
+                scalar1=mean_var[:, 0:1],
+                scalar2=inverse[:, 0:1],
+                op0=ALU.subtract,
+                op1=ALU.mult,
+            )
+            result = norm.tile([P, FEATURES], F32, name="result")
+            nc.vector.scalar_tensor_tensor(
+                out=result[:], in0=hn[:], scalar=SLOPE, in1=hn[:], op0=ALU.mult, op1=ALU.max
+            )
+            nc.sync.dma_start(out=out_rows[i], in_=result[:])
+
+        transpose_chunk(0)
+        for c in range(CHUNKS + 2):
+            if c + 1 < CHUNKS:
+                transpose_chunk(c + 1)
+            if c < CHUNKS:
+                quantise_chunk(c)
+                multiply_chunk(c)
+            if c >= 2 and c % INPUTS == 0:
+                norm_statistics(c // INPUTS - 1)
+            if c >= 3 and c % INPUTS == 1:
+                norm_apply(c // INPUTS - 1)

@@ -69,7 +69,7 @@ def tile_fcd_pa_k_kernel(tc, input1, input2, W1_words, W1_scales, b1, out):
             x_sb = resident.tile([P, K_INPUT], BF16, name="x_sb")
             x_chunks.append(x_sb)
             source = x_rows[c % INPUTS][c // INPUTS]
-            pieces = HEAD_PIECES if c == 0 else 1
+            pieces = max(1, HEAD_PIECES // 2**c)
             width = K_INPUT // pieces
             for piece in range(pieces):
                 cols = slice(piece * width, (piece + 1) * width)
@@ -87,12 +87,9 @@ def tile_fcd_pa_k_kernel(tc, input1, input2, W1_words, W1_scales, b1, out):
                     in_=W1_words.rearrange("g p c -> p g c").bitcast(I32),
                 )
 
-        bias_ps = flipped.tile([P, BANK_GROUPS, HALVES, P], F32, tag="bank")
-        nc.tensor.matmul(
-            out=bias_ps[:, 0, 0, :], lhsT=ones[:], rhs=bias_row[:], start=True, stop=True
-        )
         bias_all = const.tile([P, FEATURES], F32)
-        nc.vector.tensor_copy(out=bias_all[:], in_=bias_ps[:, 0, 0, :])
+
+        results = const.tile([P, ROW_TILES, FEATURES], F32)
 
         grouped_of = {}
         codes_of = {}
@@ -175,13 +172,17 @@ def tile_fcd_pa_k_kernel(tc, input1, input2, W1_words, W1_scales, b1, out):
                 op0=ALU.subtract,
                 op1=ALU.mult,
             )
-            result = norm.tile([P, FEATURES], F32, name="result")
             nc.vector.scalar_tensor_tensor(
-                out=result[:], in0=hn[:], scalar=SLOPE, in1=hn[:], op0=ALU.mult, op1=ALU.max
+                out=results[:, i, :], in0=hn[:], scalar=SLOPE, in1=hn[:], op0=ALU.mult, op1=ALU.max
             )
-            nc.sync.dma_start(out=out_rows[i], in_=result[:])
+            nc.sync.dma_start(out=out_rows[i], in_=results[:, i, :])
 
         transpose_chunk(0)
+        bias_ps = flipped.tile([P, BANK_GROUPS, HALVES, P], F32, tag="bank")
+        nc.tensor.matmul(
+            out=bias_ps[:, 0, 0, :], lhsT=ones[:], rhs=bias_row[:], start=True, stop=True
+        )
+        nc.vector.tensor_copy(out=bias_all[:], in_=bias_ps[:, 0, 0, :])
         for c in range(CHUNKS + 2):
             if c + 1 < CHUNKS:
                 transpose_chunk(c + 1)

@@ -28,10 +28,15 @@ ALL_GROUPS = GROUPS * INPUTS
 WORDS = K_PASS // 2
 HALVES = 2
 BANK_GROUPS = 2
+UNSORTED_GROUPS = 2
 QUANT_GROUPS = 4
 HEAD_PIECES = 4
 
 FLOPS = 2 * ROWS * K_INPUT * INPUTS * FEATURES
+
+
+def pieces_of(c):
+    return max(1, HEAD_PIECES // 2**c)
 
 
 def tile_fcd_pa_k_kernel(tc, input1, input2, W1_words, W1_scales, b1, out):
@@ -69,9 +74,8 @@ def tile_fcd_pa_k_kernel(tc, input1, input2, W1_words, W1_scales, b1, out):
             x_sb = resident.tile([P, K_INPUT], BF16, name="x_sb")
             x_chunks.append(x_sb)
             source = x_rows[c % INPUTS][c // INPUTS]
-            pieces = max(1, HEAD_PIECES // 2**c)
-            width = K_INPUT // pieces
-            for piece in range(pieces):
+            width = K_INPUT // pieces_of(c)
+            for piece in range(pieces_of(c)):
                 cols = slice(piece * width, (piece + 1) * width)
                 nc.sync.dma_start(out=x_sb[:, cols], in_=source[:, cols])
             if c == 1:
@@ -91,26 +95,44 @@ def tile_fcd_pa_k_kernel(tc, input1, input2, W1_words, W1_scales, b1, out):
 
         results = const.tile([P, ROW_TILES, FEATURES], F32)
 
+        sorted_of = {}
         grouped_of = {}
         codes_of = {}
         sum_of = {}
         h_of = {}
 
+        def sort_chunk(c):
+            x_words = x_chunks[c][:].bitcast(F32)
+            sorted_words = stage.tile([P, GROUPS, HALVES, P], F32, name="sorted_words")
+            sorted_of[c] = sorted_words
+            piece_groups = GROUPS // pieces_of(c)
+            for first in range(0, GROUPS, piece_groups):
+                low = max(first, UNSORTED_GROUPS)
+                high = first + piece_groups
+                if low < high:
+                    nc.vector.tensor_copy(
+                        out=sorted_words[:, low:high, :, :],
+                        in_=x_words[:, low * WORDS : high * WORDS].rearrange(
+                            "r (g p u) -> r g u p", p=P, u=HALVES
+                        ),
+                    )
+
         def transpose_chunk(c):
             x_words = x_chunks[c][:].bitcast(F32)
+            sorted_words = sorted_of[c]
             grouped = stage.tile([P, GROUPS, P, PACK], BF16, name="grouped", align_bytes=64)
             grouped_of[c] = grouped
             grouped_words = grouped[:].bitcast(F32)
             for first in range(0, GROUPS, BANK_GROUPS):
                 bank = flipped.tile([P, BANK_GROUPS, HALVES, P], F32, name="bank", tag="bank")
                 for j in range(BANK_GROUPS):
-                    start_word = (first + j) * WORDS
+                    g = first + j
                     for u in range(HALVES):
-                        nc.tensor.transpose(
-                            bank[:, j, u, :],
-                            x_words[:, start_word + u : start_word + WORDS : HALVES],
-                            identity[:],
-                        )
+                        if g < UNSORTED_GROUPS:
+                            words = x_words[:, g * WORDS + u : (g + 1) * WORDS : HALVES]
+                        else:
+                            words = sorted_words[:, g, u, :]
+                        nc.tensor.transpose(bank[:, j, u, :], words, identity[:])
                 nc.scalar.copy(
                     out=grouped_words[:, first : first + BANK_GROUPS, :, :],
                     in_=bank[:].rearrange("p g u r -> p g r u"),
@@ -177,7 +199,9 @@ def tile_fcd_pa_k_kernel(tc, input1, input2, W1_words, W1_scales, b1, out):
             )
             nc.sync.dma_start(out=out_rows[i], in_=results[:, i, :])
 
+        sort_chunk(0)
         transpose_chunk(0)
+        sort_chunk(1)
         bias_ps = flipped.tile([P, BANK_GROUPS, HALVES, P], F32, tag="bank")
         nc.tensor.matmul(
             out=bias_ps[:, 0, 0, :], lhsT=ones[:], rhs=bias_row[:], start=True, stop=True
@@ -188,6 +212,9 @@ def tile_fcd_pa_k_kernel(tc, input1, input2, W1_words, W1_scales, b1, out):
                 transpose_chunk(c + 1)
             if c < CHUNKS:
                 quantise_chunk(c)
+            if c + 2 < CHUNKS:
+                sort_chunk(c + 2)
+            if c < CHUNKS:
                 multiply_chunk(c)
             if c >= 2 and c % INPUTS == 0:
                 norm_statistics(c // INPUTS - 1)

@@ -28,8 +28,8 @@ ALL_GROUPS = GROUPS * INPUTS
 WORDS = K_PASS // 2
 HALVES = 2
 BANK_GROUPS = 2
-UNSORTED_GROUPS = 2
-QUANT_GROUPS = 4
+UNSORTED_GROUPS = 5
+SORTED_GROUPS = GROUPS - UNSORTED_GROUPS
 HEAD_PIECES = 4
 
 FLOPS = 2 * ROWS * K_INPUT * INPUTS * FEATURES
@@ -66,7 +66,7 @@ def tile_fcd_pa_k_kernel(tc, input1, input2, W1_words, W1_scales, b1, out):
 
         nc.scalar.dma_start(out=bias_row[0:1, :], in_=b1.rearrange("(o f) -> o f", o=1))
         warm = const.tile([P, 1], F32)
-        nc.scalar.activation(out=warm[:], in_=one[:], func=ACT.Sqrt)
+        nc.scalar.activation(out=warm[:], in_=one[:], func=ACT.Abs_reciprocal_sqrt)
 
         w_words = const.tile([P, ALL_GROUPS, 2 * FEATURES], U8, align_bytes=64)
         x_chunks = []
@@ -99,11 +99,11 @@ def tile_fcd_pa_k_kernel(tc, input1, input2, W1_words, W1_scales, b1, out):
         grouped_of = {}
         codes_of = {}
         sum_of = {}
-        h_of = {}
+        centred_of = {}
 
         def sort_chunk(c):
             x_words = x_chunks[c][:].bitcast(F32)
-            sorted_words = stage.tile([P, GROUPS, HALVES, P], F32, name="sorted_words")
+            sorted_words = stage.tile([P, HALVES, SORTED_GROUPS, P], F32, name="sorted_words")
             sorted_of[c] = sorted_words
             piece_groups = GROUPS // pieces_of(c)
             for first in range(0, GROUPS, piece_groups):
@@ -111,9 +111,9 @@ def tile_fcd_pa_k_kernel(tc, input1, input2, W1_words, W1_scales, b1, out):
                 high = first + piece_groups
                 if low < high:
                     nc.vector.tensor_copy(
-                        out=sorted_words[:, low:high, :, :],
+                        out=sorted_words[:, :, low - UNSORTED_GROUPS : high - UNSORTED_GROUPS, :],
                         in_=x_words[:, low * WORDS : high * WORDS].rearrange(
-                            "r (g p u) -> r g u p", p=P, u=HALVES
+                            "r (g p u) -> r u g p", p=P, u=HALVES
                         ),
                     )
 
@@ -131,7 +131,7 @@ def tile_fcd_pa_k_kernel(tc, input1, input2, W1_words, W1_scales, b1, out):
                         if g < UNSORTED_GROUPS:
                             words = x_words[:, g * WORDS + u : (g + 1) * WORDS : HALVES]
                         else:
-                            words = sorted_words[:, g, u, :]
+                            words = sorted_words[:, u, g - UNSORTED_GROUPS, :]
                         nc.tensor.transpose(bank[:, j, u, :], words, identity[:])
                 nc.scalar.copy(
                     out=grouped_words[:, first : first + BANK_GROUPS, :, :],
@@ -143,8 +143,8 @@ def tile_fcd_pa_k_kernel(tc, input1, input2, W1_words, W1_scales, b1, out):
             codes = stage.tile([P, GROUPS, P], U32, name="codes", align_bytes=64)
             planes = stage.tile([P, GROUPS, P], U8, name="planes", align_bytes=64)
             codes_of[c] = (codes, planes)
-            for first in range(0, GROUPS, QUANT_GROUPS):
-                some = slice(first, first + QUANT_GROUPS)
+            for first in range(0, GROUPS, BANK_GROUPS):
+                some = slice(first, first + BANK_GROUPS)
                 nc.vector.quantize_mx(
                     out=codes[:, some, :].rearrange("p g r -> p (g r)").bitcast(FP8X4),
                     scales=planes[:, some, :].rearrange("p g r -> p (g r)"),
@@ -175,27 +175,22 @@ def tile_fcd_pa_k_kernel(tc, input1, input2, W1_words, W1_scales, b1, out):
             nc.vector.bn_stats(out=stats[:], in_=h[:])
             mean_var = norm.tile([P, 2], F32, name="mean_var")
             nc.vector.bn_aggr(out=mean_var[:], in_=stats[:])
-            shifted = norm.tile([P, 1], F32, name="shifted")
-            nc.vector.tensor_scalar_add(out=shifted[:], in0=mean_var[:, 1:2], scalar1=EPS)
-            deviation = norm.tile([P, 1], F32, name="deviation")
-            nc.scalar.activation(out=deviation[:], in_=shifted[:], func=ACT.Sqrt)
-            h_of[i] = (h, mean_var, deviation)
+            centred = norm.tile([P, FEATURES], F32, name="centred")
+            nc.vector.tensor_scalar_sub(out=centred[:], in0=h[:], scalar1=mean_var[:, 0:1])
+            leaky = norm.tile([P, FEATURES], F32, name="leaky")
+            nc.vector.scalar_tensor_tensor(
+                out=leaky[:], in0=centred[:], scalar=SLOPE, in1=centred[:], op0=ALU.mult, op1=ALU.max
+            )
+            centred_of[i] = (leaky, mean_var)
 
         def norm_apply(i):
-            h, mean_var, deviation = h_of[i]
+            leaky, mean_var = centred_of[i]
             inverse = norm.tile([P, 1], F32, name="inverse")
-            nc.vector.reciprocal(out=inverse[:], in_=deviation[:])
-            hn = norm.tile([P, FEATURES], F32, name="hn")
-            nc.vector.tensor_scalar(
-                out=hn[:],
-                in0=h[:],
-                scalar1=mean_var[:, 0:1],
-                scalar2=inverse[:, 0:1],
-                op0=ALU.subtract,
-                op1=ALU.mult,
+            nc.scalar.activation(
+                out=inverse[:], in_=mean_var[:, 1:2], func=ACT.Abs_reciprocal_sqrt, bias=EPS
             )
-            nc.vector.scalar_tensor_tensor(
-                out=results[:, i, :], in0=hn[:], scalar=SLOPE, in1=hn[:], op0=ALU.mult, op1=ALU.max
+            nc.scalar.activation(
+                out=results[:, i, :], in_=leaky[:], func=ACT.Copy, scale=inverse[:, 0:1]
             )
             nc.sync.dma_start(out=out_rows[i], in_=results[:, i, :])
 

@@ -28,15 +28,30 @@ ALL_GROUPS = GROUPS * INPUTS
 WORDS = K_PASS // 2
 HALVES = 2
 BANK_GROUPS = 2
-UNSORTED_GROUPS = 5
-SORTED_GROUPS = GROUPS - UNSORTED_GROUPS
+CHUNK_BANKS = GROUPS // BANK_GROUPS
+ALL_BANKS = CHUNKS * CHUNK_BANKS
+TILE_BANKS = INPUTS * CHUNK_BANKS
+UNSORTED_BANKS = 3
+SORT_LEAD = 4
+FIRST_MULTIPLY = 15
+NORM_STAGES = 7
 HEAD_PIECES = 4
 
 FLOPS = 2 * ROWS * K_INPUT * INPUTS * FEATURES
 
 
 def pieces_of(c):
+    if c == CHUNKS - 1:
+        return 2
     return max(1, HEAD_PIECES // 2**c)
+
+
+def sorted_groups(n):
+    c, b = divmod(n, CHUNK_BANKS)
+    if c == 0:
+        return range(0)
+    first = b * BANK_GROUPS
+    return range(first + (b < UNSORTED_BANKS), first + BANK_GROUPS)
 
 
 def tile_fcd_pa_k_kernel(tc, input1, input2, W1_words, W1_scales, b1, out):
@@ -78,7 +93,7 @@ def tile_fcd_pa_k_kernel(tc, input1, input2, W1_words, W1_scales, b1, out):
             for piece in range(pieces_of(c)):
                 cols = slice(piece * width, (piece + 1) * width)
                 nc.sync.dma_start(out=x_sb[:, cols], in_=source[:, cols])
-            if c == 1:
+            if c == 2:
                 for quadrant in range(4):
                     nc.sync.dma_start(
                         out=w_planes[32 * quadrant : 32 * quadrant + 4, :, :].bitcast(I32),
@@ -99,57 +114,60 @@ def tile_fcd_pa_k_kernel(tc, input1, input2, W1_words, W1_scales, b1, out):
         grouped_of = {}
         codes_of = {}
         sum_of = {}
-        centred_of = {}
+        norm_of = {}
 
-        def sort_chunk(c):
+        def sort_bank(n):
+            groups = sorted_groups(n)
+            if len(groups) == 0:
+                return
+            c = n // CHUNK_BANKS
+            if c not in sorted_of:
+                sorted_of[c] = stage.tile([P, HALVES, GROUPS, P], F32, name="sorted_words")
             x_words = x_chunks[c][:].bitcast(F32)
-            sorted_words = stage.tile([P, HALVES, SORTED_GROUPS, P], F32, name="sorted_words")
-            sorted_of[c] = sorted_words
-            piece_groups = GROUPS // pieces_of(c)
-            for first in range(0, GROUPS, piece_groups):
-                low = max(first, UNSORTED_GROUPS)
-                high = first + piece_groups
-                if low < high:
-                    nc.vector.tensor_copy(
-                        out=sorted_words[:, :, low - UNSORTED_GROUPS : high - UNSORTED_GROUPS, :],
-                        in_=x_words[:, low * WORDS : high * WORDS].rearrange(
-                            "r (g p u) -> r u g p", p=P, u=HALVES
-                        ),
-                    )
+            nc.vector.tensor_copy(
+                out=sorted_of[c][:, :, groups.start : groups.stop, :],
+                in_=x_words[:, groups.start * WORDS : groups.stop * WORDS].rearrange(
+                    "r (g p u) -> r u g p", p=P, u=HALVES
+                ),
+            )
 
-        def transpose_chunk(c):
+        def transpose_bank(n):
+            c, b = divmod(n, CHUNK_BANKS)
             x_words = x_chunks[c][:].bitcast(F32)
-            sorted_words = sorted_of[c]
-            grouped = stage.tile([P, GROUPS, P, PACK], BF16, name="grouped", align_bytes=64)
-            grouped_of[c] = grouped
-            grouped_words = grouped[:].bitcast(F32)
-            for first in range(0, GROUPS, BANK_GROUPS):
-                bank = flipped.tile([P, BANK_GROUPS, HALVES, P], F32, name="bank", tag="bank")
-                for j in range(BANK_GROUPS):
-                    g = first + j
-                    for u in range(HALVES):
-                        if g < UNSORTED_GROUPS:
-                            words = x_words[:, g * WORDS + u : (g + 1) * WORDS : HALVES]
-                        else:
-                            words = sorted_words[:, u, g - UNSORTED_GROUPS, :]
-                        nc.tensor.transpose(bank[:, j, u, :], words, identity[:])
-                nc.scalar.copy(
-                    out=grouped_words[:, first : first + BANK_GROUPS, :, :],
-                    in_=bank[:].rearrange("p g u r -> p g r u"),
+            if b == 0:
+                grouped_of[c] = stage.tile(
+                    [P, GROUPS, P, PACK], BF16, name="grouped", align_bytes=64
                 )
+            grouped_words = grouped_of[c][:].bitcast(F32)
+            first = b * BANK_GROUPS
+            bank = flipped.tile([P, BANK_GROUPS, HALVES, P], F32, name="bank", tag="bank")
+            for j in range(BANK_GROUPS):
+                g = first + j
+                for u in range(HALVES):
+                    if g in sorted_groups(n):
+                        words = sorted_of[c][:, u, g, :]
+                    else:
+                        words = x_words[:, g * WORDS + u : (g + 1) * WORDS : HALVES]
+                    nc.tensor.transpose(bank[:, j, u, :], words, identity[:])
+            nc.scalar.copy(
+                out=grouped_words[:, first : first + BANK_GROUPS, :, :],
+                in_=bank[:].rearrange("p g u r -> p g r u"),
+            )
 
-        def quantise_chunk(c):
-            grouped = grouped_of[c]
-            codes = stage.tile([P, GROUPS, P], U32, name="codes", align_bytes=64)
-            planes = stage.tile([P, GROUPS, P], U8, name="planes", align_bytes=64)
-            codes_of[c] = (codes, planes)
-            for first in range(0, GROUPS, BANK_GROUPS):
-                some = slice(first, first + BANK_GROUPS)
-                nc.vector.quantize_mx(
-                    out=codes[:, some, :].rearrange("p g r -> p (g r)").bitcast(FP8X4),
-                    scales=planes[:, some, :].rearrange("p g r -> p (g r)"),
-                    in_=grouped[:, some, :, :].rearrange("p g r t -> p (g r t)"),
+        def quantise_bank(n):
+            c, b = divmod(n, CHUNK_BANKS)
+            if b == 0:
+                codes_of[c] = (
+                    stage.tile([P, GROUPS, P], U32, name="codes", align_bytes=64, bufs=5),
+                    stage.tile([P, GROUPS, P], U8, name="planes", align_bytes=64, bufs=5),
                 )
+            codes, planes = codes_of[c]
+            some = slice(b * BANK_GROUPS, (b + 1) * BANK_GROUPS)
+            nc.vector.quantize_mx(
+                out=codes[:, some, :].rearrange("p g r -> p (g r)").bitcast(FP8X4),
+                scales=planes[:, some, :].rearrange("p g r -> p (g r)"),
+                in_=grouped_of[c][:, some, :, :].rearrange("p g r t -> p (g r t)"),
+            )
 
         def multiply_chunk(c):
             codes, planes = codes_of[c]
@@ -168,50 +186,73 @@ def tile_fcd_pa_k_kernel(tc, input1, input2, W1_words, W1_scales, b1, out):
                     stop=(w_group == ALL_GROUPS - 1),
                 )
 
-        def norm_statistics(i):
-            h = norm.tile([P, FEATURES], F32, name="h")
-            nc.vector.tensor_tensor(out=h[:], in0=sum_of[i][:], in1=bias_all[:], op=ALU.add)
-            stats = norm.tile([P, 6], F32, name="stats")
-            nc.vector.bn_stats(out=stats[:], in_=h[:])
-            mean_var = norm.tile([P, 2], F32, name="mean_var")
-            nc.vector.bn_aggr(out=mean_var[:], in_=stats[:])
-            centred = norm.tile([P, FEATURES], F32, name="centred")
-            nc.vector.tensor_scalar_sub(out=centred[:], in0=h[:], scalar1=mean_var[:, 0:1])
-            leaky = norm.tile([P, FEATURES], F32, name="leaky")
-            nc.vector.scalar_tensor_tensor(
-                out=leaky[:], in0=centred[:], scalar=SLOPE, in1=centred[:], op0=ALU.mult, op1=ALU.max
-            )
-            centred_of[i] = (leaky, mean_var)
+        def norm_stage(i, stage_number):
+            if stage_number == 0:
+                norm_of[i] = {
+                    "h": norm.tile([P, FEATURES], F32, name="h"),
+                    "stats": norm.tile([P, 6], F32, name="stats"),
+                    "mean_var": norm.tile([P, 2], F32, name="mean_var"),
+                    "inverse": norm.tile([P, 1], F32, name="inverse"),
+                    "normed": norm.tile([P, FEATURES], F32, name="normed"),
+                }
+            t = norm_of[i]
+            if stage_number == 0:
+                nc.vector.tensor_tensor(
+                    out=t["h"][:], in0=sum_of[i][:], in1=bias_all[:], op=ALU.add
+                )
+            elif stage_number == 1:
+                nc.vector.bn_stats(out=t["stats"][:], in_=t["h"][:])
+            elif stage_number == 2:
+                nc.vector.bn_aggr(out=t["mean_var"][:], in_=t["stats"][:])
+            elif stage_number == 3:
+                nc.scalar.activation(
+                    out=t["inverse"][:],
+                    in_=t["mean_var"][:, 1:2],
+                    func=ACT.Abs_reciprocal_sqrt,
+                    bias=EPS,
+                )
+            elif stage_number == 5:
+                nc.vector.tensor_scalar(
+                    out=t["normed"][:],
+                    in0=t["h"][:],
+                    scalar1=t["mean_var"][:, 0:1],
+                    scalar2=t["inverse"][:, 0:1],
+                    op0=ALU.subtract,
+                    op1=ALU.mult,
+                )
+            elif stage_number == 6:
+                nc.vector.scalar_tensor_tensor(
+                    out=results[:, i, :],
+                    in0=t["normed"][:],
+                    scalar=SLOPE,
+                    in1=t["normed"][:],
+                    op0=ALU.mult,
+                    op1=ALU.max,
+                )
+                nc.sync.dma_start(out=out_rows[i], in_=results[:, i, :])
 
-        def norm_apply(i):
-            leaky, mean_var = centred_of[i]
-            inverse = norm.tile([P, 1], F32, name="inverse")
-            nc.scalar.activation(
-                out=inverse[:], in_=mean_var[:, 1:2], func=ACT.Abs_reciprocal_sqrt, bias=EPS
-            )
-            nc.scalar.activation(
-                out=results[:, i, :], in_=leaky[:], func=ACT.Copy, scale=inverse[:, 0:1]
-            )
-            nc.sync.dma_start(out=out_rows[i], in_=results[:, i, :])
-
-        sort_chunk(0)
-        transpose_chunk(0)
-        sort_chunk(1)
-        bias_ps = flipped.tile([P, BANK_GROUPS, HALVES, P], F32, tag="bank")
-        nc.tensor.matmul(
-            out=bias_ps[:, 0, 0, :], lhsT=ones[:], rhs=bias_row[:], start=True, stop=True
-        )
-        nc.vector.tensor_copy(out=bias_all[:], in_=bias_ps[:, 0, 0, :])
-        for c in range(CHUNKS + 2):
-            if c + 1 < CHUNKS:
-                transpose_chunk(c + 1)
-            if c < CHUNKS:
-                quantise_chunk(c)
-            if c + 2 < CHUNKS:
-                sort_chunk(c + 2)
-            if c < CHUNKS:
-                multiply_chunk(c)
-            if c >= 2 and c % INPUTS == 0:
-                norm_statistics(c // INPUTS - 1)
-            if c >= 3 and c % INPUTS == 1:
-                norm_apply(c // INPUTS - 1)
+        multiplied = 0
+        norm_due = {}
+        for n in range(ALL_BANKS + 3 * CHUNK_BANKS + 1):
+            if n < ALL_BANKS:
+                transpose_bank(n)
+            if n == CHUNK_BANKS:
+                bias_ps = flipped.tile([P, BANK_GROUPS, HALVES, P], F32, tag="bank")
+                nc.tensor.matmul(
+                    out=bias_ps[:, 0, 0, :], lhsT=ones[:], rhs=bias_row[:], start=True, stop=True
+                )
+                nc.vector.tensor_copy(out=bias_all[:], in_=bias_ps[:, 0, 0, :])
+            if 0 < n <= ALL_BANKS:
+                quantise_bank(n - 1)
+            if n + SORT_LEAD < ALL_BANKS:
+                sort_bank(n + SORT_LEAD)
+            for i, stage_number in norm_due.get(n, []):
+                norm_stage(i, stage_number)
+            if n >= FIRST_MULTIPLY and n % CHUNK_BANKS == CHUNK_BANKS - 1:
+                ready = min(CHUNKS, n // CHUNK_BANKS)
+                for c in range(multiplied, min(ready, multiplied + INPUTS)):
+                    multiply_chunk(c)
+                    multiplied = c + 1
+                    if c % INPUTS == INPUTS - 1:
+                        for s in range(NORM_STAGES):
+                            norm_due.setdefault(n + 2 + s, []).append((c // INPUTS, s))

@@ -31,9 +31,9 @@ BANK_GROUPS = 2
 CHUNK_BANKS = GROUPS // BANK_GROUPS
 ALL_BANKS = CHUNKS * CHUNK_BANKS
 TILE_BANKS = INPUTS * CHUNK_BANKS
-UNSORTED_BANKS = 3
+UNSORTED_BANKS = 4
 SORT_LEAD = 4
-FIRST_MULTIPLY = 15
+FIRST_MULTIPLY = 7
 NORM_STAGES = 7
 HEAD_PIECES = 4
 
@@ -93,7 +93,7 @@ def tile_fcd_pa_k_kernel(tc, input1, input2, W1_words, W1_scales, b1, out):
             for piece in range(pieces_of(c)):
                 cols = slice(piece * width, (piece + 1) * width)
                 nc.sync.dma_start(out=x_sb[:, cols], in_=source[:, cols])
-            if c == 2:
+            if c == 0:
                 for quadrant in range(4):
                     nc.sync.dma_start(
                         out=w_planes[32 * quadrant : 32 * quadrant + 4, :, :].bitcast(I32),
@@ -101,9 +101,11 @@ def tile_fcd_pa_k_kernel(tc, input1, input2, W1_words, W1_scales, b1, out):
                         .rearrange("g q n -> q g n")
                         .bitcast(I32),
                     )
+            if c < INPUTS:
+                groups = slice(c * GROUPS, (c + 1) * GROUPS)
                 nc.sync.dma_start(
-                    out=w_words[:].bitcast(I32),
-                    in_=W1_words.rearrange("g p c -> p g c").bitcast(I32),
+                    out=w_words[:, groups, :].bitcast(I32),
+                    in_=W1_words[groups, :, :].rearrange("g p c -> p g c").bitcast(I32),
                 )
 
         bias_all = const.tile([P, FEATURES], F32)
@@ -158,8 +160,8 @@ def tile_fcd_pa_k_kernel(tc, input1, input2, W1_words, W1_scales, b1, out):
             c, b = divmod(n, CHUNK_BANKS)
             if b == 0:
                 codes_of[c] = (
-                    stage.tile([P, GROUPS, P], U32, name="codes", align_bytes=64, bufs=5),
-                    stage.tile([P, GROUPS, P], U8, name="planes", align_bytes=64, bufs=5),
+                    stage.tile([P, GROUPS, P], U32, name="codes", align_bytes=64),
+                    stage.tile([P, GROUPS, P], U8, name="planes", align_bytes=64),
                 )
             codes, planes = codes_of[c]
             some = slice(b * BANK_GROUPS, (b + 1) * BANK_GROUPS)

@@ -28,22 +28,16 @@ ALL_GROUPS = GROUPS * INPUTS
 WORDS = K_PASS // 2
 HALVES = 2
 BANK_GROUPS = 2
+BANK_K = BANK_GROUPS * K_PASS
 CHUNK_BANKS = GROUPS // BANK_GROUPS
 ALL_BANKS = CHUNKS * CHUNK_BANKS
 TILE_BANKS = INPUTS * CHUNK_BANKS
 UNSORTED_BANKS = 4
 SORT_LEAD = 4
-FIRST_MULTIPLY = 7
+FIRST_MULTIPLY = 11
 NORM_STAGES = 7
-HEAD_PIECES = 4
 
 FLOPS = 2 * ROWS * K_INPUT * INPUTS * FEATURES
-
-
-def pieces_of(c):
-    if c == CHUNKS - 1:
-        return 2
-    return max(1, HEAD_PIECES // 2**c)
 
 
 def sorted_groups(n):
@@ -89,11 +83,10 @@ def tile_fcd_pa_k_kernel(tc, input1, input2, W1_words, W1_scales, b1, out):
             x_sb = resident.tile([P, K_INPUT], BF16, name="x_sb")
             x_chunks.append(x_sb)
             source = x_rows[c % INPUTS][c // INPUTS]
-            width = K_INPUT // pieces_of(c)
-            for piece in range(pieces_of(c)):
-                cols = slice(piece * width, (piece + 1) * width)
+            for b in range(CHUNK_BANKS):
+                cols = slice(b * BANK_K, (b + 1) * BANK_K)
                 nc.sync.dma_start(out=x_sb[:, cols], in_=source[:, cols])
-            if c == 0:
+            if c == 2:
                 for quadrant in range(4):
                     nc.sync.dma_start(
                         out=w_planes[32 * quadrant : 32 * quadrant + 4, :, :].bitcast(I32),
@@ -101,11 +94,9 @@ def tile_fcd_pa_k_kernel(tc, input1, input2, W1_words, W1_scales, b1, out):
                         .rearrange("g q n -> q g n")
                         .bitcast(I32),
                     )
-            if c < INPUTS:
-                groups = slice(c * GROUPS, (c + 1) * GROUPS)
                 nc.sync.dma_start(
-                    out=w_words[:, groups, :].bitcast(I32),
-                    in_=W1_words[groups, :, :].rearrange("g p c -> p g c").bitcast(I32),
+                    out=w_words[:].bitcast(I32),
+                    in_=W1_words.rearrange("g p c -> p g c").bitcast(I32),
                 )
 
         bias_all = const.tile([P, FEATURES], F32)
@@ -238,7 +229,7 @@ def tile_fcd_pa_k_kernel(tc, input1, input2, W1_words, W1_scales, b1, out):
         for n in range(ALL_BANKS + 3 * CHUNK_BANKS + 1):
             if n < ALL_BANKS:
                 transpose_bank(n)
-            if n == CHUNK_BANKS:
+            if n == FIRST_MULTIPLY:
                 bias_ps = flipped.tile([P, BANK_GROUPS, HALVES, P], F32, tag="bank")
                 nc.tensor.matmul(
                     out=bias_ps[:, 0, 0, :], lhsT=ones[:], rhs=bias_row[:], start=True, stop=True
@@ -252,7 +243,7 @@ def tile_fcd_pa_k_kernel(tc, input1, input2, W1_words, W1_scales, b1, out):
                 norm_stage(i, stage_number)
             if n >= FIRST_MULTIPLY and n % CHUNK_BANKS == CHUNK_BANKS - 1:
                 ready = min(CHUNKS, n // CHUNK_BANKS)
-                for c in range(multiplied, min(ready, multiplied + INPUTS)):
+                for c in range(multiplied, ready):
                     multiply_chunk(c)
                     multiplied = c + 1
                     if c % INPUTS == INPUTS - 1:

@@ -117,12 +117,13 @@ def tile_fcd_pa_k_kernel(tc, input1, input2, W1_words, W1_scales, b1, out):
             if c not in sorted_of:
                 sorted_of[c] = stage.tile([P, HALVES, GROUPS, P], F32, name="sorted_words")
             x_words = x_chunks[c][:].bitcast(F32)
-            nc.vector.tensor_copy(
-                out=sorted_of[c][:, :, groups.start : groups.stop, :],
-                in_=x_words[:, groups.start * WORDS : groups.stop * WORDS].rearrange(
-                    "r (g p u) -> r u g p", p=P, u=HALVES
-                ),
-            )
+            for g in groups:
+                nc.vector.tensor_copy(
+                    out=sorted_of[c][:, :, g, :].rearrange("r u (h p) -> r h u p", h=2),
+                    in_=x_words[:, g * WORDS : (g + 1) * WORDS].rearrange(
+                        "r (h p u) -> r h u p", h=2, u=HALVES
+                    ),
+                )
 
         def transpose_bank(n):
             c, b = divmod(n, CHUNK_BANKS)

@@ -87,12 +87,10 @@ def tile_fcd_pa_k_kernel(tc, input1, input2, W1_words, W1_scales, b1, out):
                 cols = slice(b * BANK_K, (b + 1) * BANK_K)
                 nc.sync.dma_start(out=x_sb[:, cols], in_=source[:, cols])
             if c == 2:
-                for quadrant in range(4):
+                for r in range(4):
                     nc.sync.dma_start(
-                        out=w_planes[32 * quadrant : 32 * quadrant + 4, :, :].bitcast(I32),
-                        in_=W1_scales[:, 4 * quadrant : 4 * quadrant + 4, :]
-                        .rearrange("g q n -> q g n")
-                        .bitcast(I32),
+                        out=w_planes[r:P:32, :, :].bitcast(I32),
+                        in_=W1_scales[:, r:16:4, :].rearrange("g q n -> q g n").bitcast(I32),
                     )
                 nc.sync.dma_start(
                     out=w_words[:].bitcast(I32),
@@ -163,12 +161,12 @@ def tile_fcd_pa_k_kernel(tc, input1, input2, W1_words, W1_scales, b1, out):
                 in_=grouped_of[c][:, some, :, :].rearrange("p g r t -> p (g r t)"),
             )
 
-        def multiply_chunk(c):
+        def multiply(c, groups):
             codes, planes = codes_of[c]
-            if c % INPUTS == 0:
+            if c % INPUTS == 0 and groups[0] == 0:
                 sum_of[c // INPUTS] = sums.tile([P, FEATURES], F32, name="total")
             total = sum_of[c // INPUTS]
-            for g in range(GROUPS):
+            for g in groups:
                 w_group = (c % INPUTS) * GROUPS + g
                 nc.tensor.matmul_mx(
                     out=total[:],
@@ -236,17 +234,21 @@ def tile_fcd_pa_k_kernel(tc, input1, input2, W1_words, W1_scales, b1, out):
                     out=bias_ps[:, 0, 0, :], lhsT=ones[:], rhs=bias_row[:], start=True, stop=True
                 )
                 nc.vector.tensor_copy(out=bias_all[:], in_=bias_ps[:, 0, 0, :])
+            for i, stage_number in norm_due.get(n, []):
+                norm_stage(i, stage_number)
             if 0 < n <= ALL_BANKS:
                 quantise_bank(n - 1)
             if n + SORT_LEAD < ALL_BANKS:
                 sort_bank(n + SORT_LEAD)
-            for i, stage_number in norm_due.get(n, []):
-                norm_stage(i, stage_number)
+            if n == ALL_BANKS:
+                multiply(CHUNKS - 1, range(GROUPS - BANK_GROUPS))
+                multiply(CHUNKS - 1, range(GROUPS - BANK_GROUPS, GROUPS))
             if n >= FIRST_MULTIPLY and n % CHUNK_BANKS == CHUNK_BANKS - 1:
                 ready = min(CHUNKS, n // CHUNK_BANKS)
                 for c in range(multiplied, ready):
-                    multiply_chunk(c)
+                    if c < CHUNKS - 1:
+                        multiply(c, range(GROUPS))
                     multiplied = c + 1
                     if c % INPUTS == INPUTS - 1:
                         for s in range(NORM_STAGES):
-                            norm_due.setdefault(n + 2 + s, []).append((c // INPUTS, s))
+                            norm_due.setdefault(n + 1 + s, []).append((c // INPUTS, s))

@@ -32,8 +32,8 @@ BANK_K = BANK_GROUPS * K_PASS
 CHUNK_BANKS = GROUPS // BANK_GROUPS
 ALL_BANKS = CHUNKS * CHUNK_BANKS
 TILE_BANKS = INPUTS * CHUNK_BANKS
-UNSORTED_BANKS = 4
-SORT_LEAD = 4
+SORTED_OF_BANK = (2, 1, 1, 0)
+SORT_LEAD = 3
 FIRST_MULTIPLY = 11
 NORM_STAGES = 7
 
@@ -42,10 +42,8 @@ FLOPS = 2 * ROWS * K_INPUT * INPUTS * FEATURES
 
 def sorted_groups(n):
     c, b = divmod(n, CHUNK_BANKS)
-    if c == 0:
-        return range(0)
-    first = b * BANK_GROUPS
-    return range(first + (b < UNSORTED_BANKS), first + BANK_GROUPS)
+    end = (b + 1) * BANK_GROUPS
+    return range(end - (SORTED_OF_BANK[b] if c > 0 else 0), end)
 
 
 def tile_fcd_pa_k_kernel(tc, input1, input2, W1_words, W1_scales, b1, out):
@@ -113,14 +111,18 @@ def tile_fcd_pa_k_kernel(tc, input1, input2, W1_words, W1_scales, b1, out):
                 return
             c = n // CHUNK_BANKS
             if c not in sorted_of:
-                sorted_of[c] = stage.tile([P, HALVES, GROUPS, P], F32, name="sorted_words")
-            x_words = x_chunks[c][:].bitcast(F32)
-            for g in groups:
+                sorted_of[c] = stage.tile([P, GROUPS, HALVES, P], F32, name="sorted_words")
+            x_words = x_chunks[c][:, groups.start * K_PASS : groups.stop * K_PASS].bitcast(F32)
+            sorted_words = sorted_of[c][:, groups.start : groups.stop, :, :]
+            if len(groups) == 1:
                 nc.vector.tensor_copy(
-                    out=sorted_of[c][:, :, g, :].rearrange("r u (h p) -> r h u p", h=2),
-                    in_=x_words[:, g * WORDS : (g + 1) * WORDS].rearrange(
-                        "r (h p u) -> r h u p", h=2, u=HALVES
-                    ),
+                    out=sorted_words.rearrange("r g u (h p) -> r (g h) u p", h=2),
+                    in_=x_words.rearrange("r (h p u) -> r h u p", h=2, u=HALVES),
+                )
+            else:
+                nc.vector.tensor_copy(
+                    out=sorted_words,
+                    in_=x_words.rearrange("r (g p u) -> r g u p", p=P, u=HALVES),
                 )
 
         def transpose_bank(n):
@@ -137,7 +139,7 @@ def tile_fcd_pa_k_kernel(tc, input1, input2, W1_words, W1_scales, b1, out):
                 g = first + j
                 for u in range(HALVES):
                     if g in sorted_groups(n):
-                        words = sorted_of[c][:, u, g, :]
+                        words = sorted_of[c][:, g, u, :]
                     else:
                         words = x_words[:, g * WORDS + u : (g + 1) * WORDS : HALVES]
                     nc.tensor.transpose(bank[:, j, u, :], words, identity[:])
@@ -226,6 +228,8 @@ def tile_fcd_pa_k_kernel(tc, input1, input2, W1_words, W1_scales, b1, out):
         multiplied = 0
         norm_due = {}
         for n in range(ALL_BANKS + 3 * CHUNK_BANKS + 1):
+            if n + SORT_LEAD < ALL_BANKS:
+                sort_bank(n + SORT_LEAD)
             if n < ALL_BANKS:
                 transpose_bank(n)
             if n == FIRST_MULTIPLY:
@@ -238,8 +242,6 @@ def tile_fcd_pa_k_kernel(tc, input1, input2, W1_words, W1_scales, b1, out):
                 norm_stage(i, stage_number)
             if 0 < n <= ALL_BANKS:
                 quantise_bank(n - 1)
-            if n + SORT_LEAD < ALL_BANKS:
-                sort_bank(n + SORT_LEAD)
             if n == ALL_BANKS:
                 multiply(CHUNKS - 1, range(GROUPS - BANK_GROUPS))
                 multiply(CHUNKS - 1, range(GROUPS - BANK_GROUPS, GROUPS))

@@ -34,6 +34,7 @@ ALL_BANKS = CHUNKS * CHUNK_BANKS
 TILE_BANKS = INPUTS * CHUNK_BANKS
 SORTED_OF_BANK = (2, 1, 1, 0)
 SORT_LEAD = 3
+W_CHUNK = 3
 FIRST_MULTIPLY = 11
 NORM_STAGES = 7
 
@@ -81,10 +82,12 @@ def tile_fcd_pa_k_kernel(tc, input1, input2, W1_words, W1_scales, b1, out):
             x_sb = resident.tile([P, K_INPUT], BF16, name="x_sb")
             x_chunks.append(x_sb)
             source = x_rows[c % INPUTS][c // INPUTS]
-            for b in range(CHUNK_BANKS):
-                cols = slice(b * BANK_K, (b + 1) * BANK_K)
+            pieces = CHUNK_BANKS // 2 if c < W_CHUNK else CHUNK_BANKS
+            width = K_INPUT // pieces
+            for b in range(pieces):
+                cols = slice(b * width, (b + 1) * width)
                 nc.sync.dma_start(out=x_sb[:, cols], in_=source[:, cols])
-            if c == 2:
+            if c == W_CHUNK - 1:
                 for r in range(4):
                     nc.sync.dma_start(
                         out=w_planes[r:P:32, :, :].bitcast(I32),

import concourse.mybir as mybir
from concourse.masks import make_identity

F32 = mybir.dt.float32
BF16 = mybir.dt.bfloat16
I32 = mybir.dt.int32
U32 = mybir.dt.uint32
U8 = mybir.dt.uint8
FP8X4 = mybir.dt.float8_e4m3fn_x4
FP4X4 = mybir.dt.float4_e2m1fn_x4
ALU = mybir.AluOpType
ACT = mybir.ActivationFunctionType

P = 128
PACK = 4
K_PASS = P * PACK
ROWS = 1024
K_INPUT = 4096
FEATURES = 128
EPS = 1e-5
SLOPE = 0.2

ROW_TILES = ROWS // P
INPUTS = 2
CHUNKS = ROW_TILES * INPUTS
GROUPS = K_INPUT // K_PASS
ALL_GROUPS = GROUPS * INPUTS
WORDS = K_PASS // 2
HALVES = 2
BANK_GROUPS = 2
BANK_K = BANK_GROUPS * K_PASS
CHUNK_BANKS = GROUPS // BANK_GROUPS
ALL_BANKS = CHUNKS * CHUNK_BANKS
TILE_BANKS = INPUTS * CHUNK_BANKS
SORTED_OF_BANK = (2, 1, 1, 0)
SORT_LEAD = 3
W_CHUNK = 3
FIRST_MULTIPLY = 11
NORM_STAGES = 7

FLOPS = 2 * ROWS * K_INPUT * INPUTS * FEATURES


def sorted_groups(n):
    c, b = divmod(n, CHUNK_BANKS)
    end = (b + 1) * BANK_GROUPS
    return range(end - (SORTED_OF_BANK[b] if c > 0 else 0), end)


def tile_fcd_pa_k_kernel(tc, input1, input2, W1_words, W1_scales, b1, out):
    nc = tc.nc
    x_rows = [
        source.rearrange("(i p) o k -> i p (o k)", p=P) for source in (input1, input2)
    ]
    out_rows = out.rearrange("(i p) o f -> i p (o f)", p=P)

    with tc.tile_pool(name="const", bufs=1) as const, tc.tile_pool(
        name="resident", bufs=CHUNKS
    ) as resident, tc.tile_pool(name="stage", bufs=3) as stage, tc.tile_pool(
        name="norm", bufs=2
    ) as norm, tc.psum_pool(name="flipped", bufs=6) as flipped, tc.psum_pool(
        name="sums", bufs=2
    ) as sums, tc.manual_schedule():
        w_planes = const.tile([P, ALL_GROUPS, FEATURES], U8, align_bytes=64)
        nc.vector.memset(w_planes[:].bitcast(I32), 0)
        bias_row = const.tile([P, FEATURES], BF16)
        nc.vector.memset(bias_row[:], 0.0)
        ones = const.tile([P, P], BF16)
        nc.vector.memset(ones[:], 1.0)
        one = const.tile([P, 1], F32)
        nc.vector.memset(one[:], 1.0)
        identity = const.tile([P, P], F32)
        make_identity(nc, identity[:])

        nc.scalar.dma_start(out=bias_row[0:1, :], in_=b1.rearrange("(o f) -> o f", o=1))
        warm = const.tile([P, 1], F32)
        nc.scalar.activation(out=warm[:], in_=one[:], func=ACT.Abs_reciprocal_sqrt)

        w_words = const.tile([P, ALL_GROUPS, 2 * FEATURES], U8, align_bytes=64)
        x_chunks = []
        for c in range(CHUNKS):
            x_sb = resident.tile([P, K_INPUT], BF16, name="x_sb")
            x_chunks.append(x_sb)
            source = x_rows[c % INPUTS][c // INPUTS]
            pieces = CHUNK_BANKS // 2 if c < W_CHUNK else CHUNK_BANKS
            width = K_INPUT // pieces
            for b in range(pieces):
                cols = slice(b * width, (b + 1) * width)
                nc.sync.dma_start(out=x_sb[:, cols], in_=source[:, cols])
            if c == W_CHUNK - 1:
                for r in range(4):
                    nc.sync.dma_start(
                        out=w_planes[r:P:32, :, :].bitcast(I32),
                        in_=W1_scales[:, r:16:4, :].rearrange("g q n -> q g n").bitcast(I32),
                    )
                nc.sync.dma_start(
                    out=w_words[:].bitcast(I32),
                    in_=W1_words.rearrange("g p c -> p g c").bitcast(I32),
                )

        bias_all = const.tile([P, FEATURES], F32)

        results = const.tile([P, ROW_TILES, FEATURES], F32)

        sorted_of = {}
        grouped_of = {}
        codes_of = {}
        sum_of = {}
        norm_of = {}

        def sort_bank(n):
            groups = sorted_groups(n)
            if len(groups) == 0:
                return
            c = n // CHUNK_BANKS
            if c not in sorted_of:
                sorted_of[c] = stage.tile([P, GROUPS, HALVES, P], F32, name="sorted_words")
            x_words = x_chunks[c][:, groups.start * K_PASS : groups.stop * K_PASS].bitcast(F32)
            sorted_words = sorted_of[c][:, groups.start : groups.stop, :, :]
            if len(groups) == 1:
                nc.vector.tensor_copy(
                    out=sorted_words.rearrange("r g u (h p) -> r (g h) u p", h=2),
                    in_=x_words.rearrange("r (h p u) -> r h u p", h=2, u=HALVES),
                )
            else:
                nc.vector.tensor_copy(
                    out=sorted_words,
                    in_=x_words.rearrange("r (g p u) -> r g u p", p=P, u=HALVES),
                )

        def transpose_bank(n):
            c, b = divmod(n, CHUNK_BANKS)
            x_words = x_chunks[c][:].bitcast(F32)
            if b == 0:
                grouped_of[c] = stage.tile(
                    [P, GROUPS, P, PACK], BF16, name="grouped", align_bytes=64
                )
            grouped_words = grouped_of[c][:].bitcast(F32)
            first = b * BANK_GROUPS
            bank = flipped.tile([P, BANK_GROUPS, HALVES, P], F32, name="bank", tag="bank")
            for j in range(BANK_GROUPS):
                g = first + j
                for u in range(HALVES):
                    if g in sorted_groups(n):
                        words = sorted_of[c][:, g, u, :]
                    else:
                        words = x_words[:, g * WORDS + u : (g + 1) * WORDS : HALVES]
                    nc.tensor.transpose(bank[:, j, u, :], words, identity[:])
            nc.scalar.copy(
                out=grouped_words[:, first : first + BANK_GROUPS, :, :],
                in_=bank[:].rearrange("p g u r -> p g r u"),
            )

        def quantise_bank(n):
            c, b = divmod(n, CHUNK_BANKS)
            if b == 0:
                codes_of[c] = (
                    stage.tile([P, GROUPS, P], U32, name="codes", align_bytes=64),
                    stage.tile([P, GROUPS, P], U8, name="planes", align_bytes=64),
                )
            codes, planes = codes_of[c]
            some = slice(b * BANK_GROUPS, (b + 1) * BANK_GROUPS)
            nc.vector.quantize_mx(
                out=codes[:, some, :].rearrange("p g r -> p (g r)").bitcast(FP8X4),
                scales=planes[:, some, :].rearrange("p g r -> p (g r)"),
                in_=grouped_of[c][:, some, :, :].rearrange("p g r t -> p (g r t)"),
            )

        def multiply(c, groups):
            codes, planes = codes_of[c]
            if c % INPUTS == 0 and groups[0] == 0:
                sum_of[c // INPUTS] = sums.tile([P, FEATURES], F32, name="total")
            total = sum_of[c // INPUTS]
            for g in groups:
                w_group = (c % INPUTS) * GROUPS + g
                nc.tensor.matmul_mx(
                    out=total[:],
                    lhsT=codes[:, g, :].bitcast(FP8X4),
                    lhsT_scale=planes[:, g, :],
                    rhs=w_words[:, w_group, :].bitcast(FP4X4),
                    rhs_scale=w_planes[:, w_group, :],
                    start=(w_group == 0),
                    stop=(w_group == ALL_GROUPS - 1),
                )

        def norm_stage(i, stage_number):
            if stage_number == 0:
                norm_of[i] = {
                    "h": norm.tile([P, FEATURES], F32, name="h"),
                    "stats": norm.tile([P, 6], F32, name="stats"),
                    "mean_var": norm.tile([P, 2], F32, name="mean_var"),
                    "inverse": norm.tile([P, 1], F32, name="inverse"),
                    "normed": norm.tile([P, FEATURES], F32, name="normed"),
                }
            t = norm_of[i]
            if stage_number == 0:
                nc.vector.tensor_tensor(
                    out=t["h"][:], in0=sum_of[i][:], in1=bias_all[:], op=ALU.add
                )
            elif stage_number == 1:
                nc.vector.bn_stats(out=t["stats"][:], in_=t["h"][:])
            elif stage_number == 2:
                nc.vector.bn_aggr(out=t["mean_var"][:], in_=t["stats"][:])
            elif stage_number == 3:
                nc.scalar.activation(
                    out=t["inverse"][:],
                    in_=t["mean_var"][:, 1:2],
                    func=ACT.Abs_reciprocal_sqrt,
                    bias=EPS,
                )
            elif stage_number == 5:
                nc.vector.tensor_scalar(
                    out=t["normed"][:],
                    in0=t["h"][:],
                    scalar1=t["mean_var"][:, 0:1],
                    scalar2=t["inverse"][:, 0:1],
                    op0=ALU.subtract,
                    op1=ALU.mult,
                )
            elif stage_number == 6:
                nc.vector.scalar_tensor_tensor(
                    out=results[:, i, :],
                    in0=t["normed"][:],
                    scalar=SLOPE,
                    in1=t["normed"][:],
                    op0=ALU.mult,
                    op1=ALU.max,
                )
                nc.sync.dma_start(out=out_rows[i], in_=results[:, i, :])

        multiplied = 0
        norm_due = {}
        for n in range(ALL_BANKS + 3 * CHUNK_BANKS + 1):
            if n + SORT_LEAD < ALL_BANKS:
                sort_bank(n + SORT_LEAD)
            if n < ALL_BANKS:
                transpose_bank(n)
            if n == FIRST_MULTIPLY:
                bias_ps = flipped.tile([P, BANK_GROUPS, HALVES, P], F32, tag="bank")
                nc.tensor.matmul(
                    out=bias_ps[:, 0, 0, :], lhsT=ones[:], rhs=bias_row[:], start=True, stop=True
                )
                nc.vector.tensor_copy(out=bias_all[:], in_=bias_ps[:, 0, 0, :])
            for i, stage_number in norm_due.get(n, []):
                norm_stage(i, stage_number)
            if 0 < n <= ALL_BANKS:
                quantise_bank(n - 1)
            if n == ALL_BANKS:
                multiply(CHUNKS - 1, range(GROUPS - BANK_GROUPS))
                multiply(CHUNKS - 1, range(GROUPS - BANK_GROUPS, GROUPS))
            if n >= FIRST_MULTIPLY and n % CHUNK_BANKS == CHUNK_BANKS - 1:
                ready = min(CHUNKS, n // CHUNK_BANKS)
                for c in range(multiplied, ready):
                    if c < CHUNKS - 1:
                        multiply(c, range(GROUPS))
                    multiplied = c + 1
                    if c % INPUTS == INPUTS - 1:
                        for s in range(NORM_STAGES):
                            norm_due.setdefault(n + 1 + s, []).append((c // INPUTS, s))
